import numpy as np
import ml_dtypes


def mxq(x, axis, fmt="e4m3"):
    dtype, down = {"e4m3": (ml_dtypes.float8_e4m3fn, 7), "e5m2": (ml_dtypes.float8_e5m2, 14)}[fmt]
    v = np.moveaxis(np.asarray(x, np.float32).astype(ml_dtypes.bfloat16).astype(np.float64), axis, -1)
    blocks = v.reshape(v.shape[:-1] + (-1, 32))
    amax = np.abs(blocks).max(-1, keepdims=True)
    byte = np.maximum(np.where(amax > 0, np.frexp(amax)[1] - 1 + 127, 0) - down, 1)
    scale = np.exp2(byte - 127.0)
    codes = (blocks / scale).astype(np.float32).astype(dtype).astype(np.float64)
    return np.moveaxis((codes * scale).reshape(v.shape), -1, axis)


WIDE = False


def mx_kscale(k):
    if not WIDE:
        return np.ones(k)
    levels = np.array([10, -10, 5, -5, 0])
    a = np.random.permutation(np.resize(levels, k // 512 * 4)).reshape(k // 512, 4)
    idx = np.arange(k)
    return np.exp2(a[idx // 512, idx % 128 // 32])


BF16 = ml_dtypes.bfloat16


def bf(x):
    return np.asarray(x, np.float32).astype(BF16)


def f64(x):
    return np.asarray(x).astype(np.float64)


E2M1 = np.array([0.0, 0.5, 1.0, 1.5, 2.0, 3.0, 4.0, 6.0, -0.0, -0.5, -1.0, -1.5, -2.0, -3.0, -4.0, -6.0])


def pack_weight(w, fmt):
    k, n = w.shape
    w = f64(bf(w)).reshape(k // 32, 32, n)
    amax = np.abs(w).max(1)
    if fmt == "e4m3":
        byte = np.frexp(amax)[1] - 1 + 127 - 7
    else:
        mant, ex = np.frexp(amax / 6.0)
        byte = np.where(mant > 0.5, ex, ex - 1) + 127
    byte = np.clip(np.where(amax > 0, byte, 1), 1, 254)
    scaled = (w * np.exp2(127.0 - byte)[:, None, :]).reshape(k, n).astype(np.float32)
    by_word = np.ascontiguousarray(scaled.reshape(k // 512, 128, 4, n).transpose(0, 1, 3, 2))
    if fmt == "e4m3":
        words = by_word.astype(ml_dtypes.float8_e4m3fn).view(np.uint8)
    else:
        c = by_word.astype(ml_dtypes.float4_e2m1fn).view(np.uint8) & 0xF
        words = c[..., 0::2] | (c[..., 1::2] << 4)
    return np.ascontiguousarray(words), np.ascontiguousarray(byte.astype(np.uint8).reshape(k // 512, 16, n))


def unpack_weight(words, scales, fmt):
    g, p, n, _ = words.shape
    if fmt == "e4m3":
        vals = np.ascontiguousarray(words).view(ml_dtypes.float8_e4m3fn).astype(np.float64)
    else:
        nib = np.empty((g, p, n, 4), np.uint8)
        nib[..., 0::2] = words & 0xF
        nib[..., 1::2] = words >> 4
        vals = E2M1[nib]
    vals = vals * np.repeat(np.exp2(scales.astype(np.float64) - 127.0), 8, axis=1)[..., None]
    return vals.transpose(0, 1, 3, 2).reshape(g * 512, n)


B, D_IN, D_H = 128, 16384, 512
FMT = "e4m3"


def setup_inputs():
    s, t = mx_kscale(D_IN), mx_kscale(D_H)
    inp = {"x": bf(np.random.standard_normal((B, D_IN)) * s),
           "h_prev": bf(np.random.standard_normal((B, D_H)) * t),
           "c_prev": bf(np.random.standard_normal((B, D_H))),
           "n_prev": bf(np.random.uniform(size=(B, D_H)))}
    for g in ("i", "f", "z"):
        words, scales = pack_weight(np.random.standard_normal((D_IN, D_H)) * 0.5 / np.sqrt(D_IN) / s[:, None], FMT)
        inp["W_" + g + "_words"] = words
        inp["W_" + g + "_scales"] = scales
        inp["b_" + g] = bf(np.random.standard_normal(D_H) * 0.3)
        words, scales = pack_weight(np.random.standard_normal((D_H, D_H)) * 0.5 / np.sqrt(D_H) / t[:, None], FMT)
        inp["U_" + g + "_words"] = words
        inp["U_" + g + "_scales"] = scales
    return inp


def reference(x, h_prev, c_prev, n_prev, W_i_words, W_i_scales, b_i, U_i_words, U_i_scales, W_f_words, W_f_scales, b_f, U_f_words, U_f_scales, W_z_words, W_z_scales, b_z, U_z_words, U_z_scales):
    xq = mxq(f64(x), 1, "e4m3")
    hq = mxq(f64(h_prev), 1, "e4m3")
    i = np.exp((xq @ unpack_weight(W_i_words, W_i_scales, FMT)) + f64(b_i) + (hq @ unpack_weight(U_i_words, U_i_scales, FMT)))
    f = np.exp((xq @ unpack_weight(W_f_words, W_f_scales, FMT)) + f64(b_f) + (hq @ unpack_weight(U_f_words, U_f_scales, FMT)))
    z = np.tanh((xq @ unpack_weight(W_z_words, W_z_scales, FMT)) + f64(b_z) + (hq @ unpack_weight(U_z_words, U_z_scales, FMT)))
    c = f * f64(c_prev) + i * z
    n = f * f64(n_prev) + i
    return (c, n)

@@ -1,0 +1,233 @@
+from contextlib import ExitStack
+
+import concourse.mybir as mybir
+from concourse.masks import make_identity
+
+F32 = mybir.dt.float32
+BF16 = mybir.dt.bfloat16
+I32 = mybir.dt.int32
+U32 = mybir.dt.uint32
+U8 = mybir.dt.uint8
+FP8X4 = mybir.dt.float8_e4m3fn_x4
+ADD = mybir.AluOpType.add
+MULT = mybir.AluOpType.mult
+EXP = mybir.ActivationFunctionType.Exp
+TANH = mybir.ActivationFunctionType.Tanh
+
+P = 128
+BATCH = 128
+D_IN = 16384
+D_H = 512
+GATES = 3
+K_PASS = 4 * P
+X_PASSES = D_IN // K_PASS
+PASSES_PER_LOAD = 4
+LOADS = X_PASSES // PASSES_PER_LOAD
+WORDS_PER_PASS = K_PASS // 2
+W_BUFFERS = 12
+HALF = D_H // 2
+
+FLOPS = 2 * BATCH * (D_IN + D_H) * D_H * GATES
+
+
+def tile_slstmcell_pa_k_kernel(
+    tc,
+    x,
+    h_prev,
+    c_prev,
+    n_prev,
+    W_i_words,
+    W_i_scales,
+    b_i,
+    U_i_words,
+    U_i_scales,
+    W_f_words,
+    W_f_scales,
+    b_f,
+    U_f_words,
+    U_f_scales,
+    W_z_words,
+    W_z_scales,
+    b_z,
+    U_z_words,
+    U_z_scales,
+    out_0,
+    out_1,
+):
+    nc = tc.nc
+    w_words = (W_i_words, W_f_words, W_z_words)
+    w_scales = (W_i_scales, W_f_scales, W_z_scales)
+    u_words = (U_i_words, U_f_words, U_z_words)
+    u_scales = (U_i_scales, U_f_scales, U_z_scales)
+    biases = (b_i, b_f, b_z)
+
+    with ExitStack() as ctx:
+        ctx.enter_context(tc.manual_schedule())
+        keep = ctx.enter_context(tc.tile_pool(name="keep", bufs=1))
+        x_pool = ctx.enter_context(tc.tile_pool(name="x_pool", bufs=LOADS))
+        grouped_pool = ctx.enter_context(tc.tile_pool(name="grouped_pool", bufs=3))
+        w_pool = ctx.enter_context(tc.tile_pool(name="w_pool", bufs=W_BUFFERS))
+        bank_pool = ctx.enter_context(tc.psum_pool(name="bank_pool", bufs=4))
+        acc_pool = ctx.enter_context(tc.psum_pool(name="acc_pool", bufs=GATES))
+
+        w_planes = keep.tile([P, GATES, LOADS, D_H], U8, align_bytes=64)
+        u_planes = keep.tile([P, D_H], U8, align_bytes=64)
+        nc.vector.memset(u_planes[:].bitcast(I32), 0)
+        for gate in range(GATES):
+            nc.vector.memset(w_planes[:, gate, :, :].bitcast(I32), 0)
+
+        bias_rows = keep.tile([P, GATES, D_H], BF16)
+        ones = keep.tile([P, P], BF16)
+        nc.vector.memset(bias_rows[:], 0.0)
+        nc.vector.memset(ones[:], 1.0)
+
+        identity = keep.tile([P, P], F32)
+        make_identity(nc, identity[:])
+
+        for gate in range(GATES):
+            for quad in range(4):
+                first = 32 * quad + 4 * gate
+                nc.gpsimd.dma_start(
+                    out=u_planes[first : first + 4, :].bitcast(F32),
+                    in_=u_scales[gate][0, 4 * quad : 4 * quad + 4, :].bitcast(F32),
+                )
+            for quad in range(4):
+                for row in range(4):
+                    first = 32 * quad + row
+                    nc.gpsimd.dma_start(
+                        out=w_planes[first : first + 16 : 4, gate, :, :].bitcast(F32),
+                        in_=w_scales[gate][:, 4 * quad + row, :]
+                        .rearrange("(s j) n -> j s n", j=PASSES_PER_LOAD)
+                        .bitcast(F32),
+                    )
+
+        h_rows = keep.tile([BATCH, D_H], BF16)
+        nc.sync.dma_start(out=h_rows[:], in_=h_prev[:, :])
+        x_rows = []
+        for load in range(LOADS):
+            rows = x_pool.tile([BATCH, PASSES_PER_LOAD * K_PASS], BF16, name="rows")
+            first = load * PASSES_PER_LOAD * K_PASS
+            nc.sync.dma_start(out=rows[:], in_=x[:, first : first + PASSES_PER_LOAD * K_PASS])
+            x_rows.append(rows)
+        for gate in range(GATES):
+            nc.sync.dma_start(
+                out=bias_rows[0:1, gate, :], in_=biases[gate].rearrange("(o n) -> o n", o=1)
+            )
+        c_old = keep.tile([BATCH, D_H], BF16)
+        n_old = keep.tile([BATCH, D_H], BF16)
+        nc.sync.dma_start(out=c_old[:], in_=c_prev[:, :])
+        nc.sync.dma_start(out=n_old[:], in_=n_prev[:, :])
+        u_tile = keep.tile([P, GATES, 4 * D_H], U8, align_bytes=64)
+        for gate in range(GATES):
+            nc.sync.dma_start(
+                out=u_tile[:, gate, :].bitcast(I32),
+                in_=u_words[gate][0].rearrange("p n t -> p (n t)").bitcast(I32),
+            )
+
+        h_codes = keep.tile([P, BATCH], U32, align_bytes=64)
+        h_plane = keep.tile([P, BATCH], U8, align_bytes=64)
+        x_codes = keep.tile([P, X_PASSES, BATCH], U32, align_bytes=64)
+        x_planes = keep.tile([P, X_PASSES, BATCH], U8, align_bytes=64)
+
+        def regroup(rows, first_pass, passes, copy, grouped_words):
+            words = rows.bitcast(F32)
+            bank = bank_pool.tile([P, passes, 2, BATCH], F32, tag="bank")
+            for g in range(passes):
+                start = (first_pass + g) * WORDS_PER_PASS
+                for u in range(2):
+                    nc.tensor.transpose(
+                        bank[:, g, u, :], words[:, start + u : start + WORDS_PER_PASS : 2], identity[:]
+                    )
+            copy(
+                out=grouped_words.rearrange("p (g b u) -> p g b u", g=passes, u=2),
+                in_=bank[:].rearrange("p g u b -> p g b u"),
+            )
+
+        def quantise(grouped, codes, plane):
+            nc.vector.quantize_mx(out=codes.bitcast(FP8X4), scales=plane, in_=grouped)
+
+        h_grouped = keep.tile([P, K_PASS], BF16, align_bytes=64)
+        regroup(h_rows[:], 0, 1, nc.vector.tensor_copy, h_grouped[:].bitcast(F32))
+        waiting = (h_grouped[:], h_codes[:], h_plane[:])
+        for load in range(LOADS):
+            grouped = grouped_pool.tile([P, PASSES_PER_LOAD * K_PASS], BF16, align_bytes=64)
+            grouped_words = grouped[:].bitcast(F32)
+            regroup(x_rows[load][:], 0, 2, nc.vector.tensor_copy, grouped_words[:, 0:K_PASS])
+            regroup(x_rows[load][:], 2, 2, nc.scalar.copy, grouped_words[:, K_PASS : 2 * K_PASS])
+            quantise(*waiting)
+            passes = slice(load * PASSES_PER_LOAD, (load + 1) * PASSES_PER_LOAD)
+            waiting = (
+                grouped[:],
+                x_codes[:, passes, :].rearrange("p g b -> p (g b)"),
+                x_planes[:, passes, :].rearrange("p g b -> p (g b)"),
+            )
+        quantise(*waiting)
+
+        bias = keep.tile([BATCH, GATES, D_H], F32)
+        for gate in range(GATES):
+            spread = bank_pool.tile([BATCH, D_H], F32, tag="bank")
+            nc.tensor.matmul(spread[:], lhsT=ones[:], rhs=bias_rows[:, gate, :], start=True, stop=True)
+            nc.scalar.copy(out=bias[:, gate, :], in_=spread[:])
+
+        def products(gate):
+            acc = acc_pool.tile([BATCH, D_H], F32, tag="acc")
+            nc.tensor.matmul_mx(
+                out=acc[:],
+                lhsT=h_codes[:].bitcast(FP8X4),
+                lhsT_scale=h_plane[:],
+                rhs=u_tile[:, gate, :].bitcast(FP8X4),
+                rhs_scale=u_planes[4 * gate : P, :],
+                start=True,
+                stop=False,
+            )
+            for load in range(LOADS):
+                w_tile = w_pool.tile([P, PASSES_PER_LOAD, 4 * D_H], U8, align_bytes=64)
+                first = load * PASSES_PER_LOAD
+                nc.sync.dma_start(
+                    out=w_tile[:].bitcast(I32),
+                    in_=w_words[gate][first : first + PASSES_PER_LOAD]
+                    .rearrange("g p n t -> p g (n t)")
+                    .bitcast(I32),
+                )
+                for j in range(PASSES_PER_LOAD):
+                    nc.tensor.matmul_mx(
+                        out=acc[:],
+                        lhsT=x_codes[:, first + j, :].bitcast(FP8X4),
+                        lhsT_scale=x_planes[:, first + j, :],
+                        rhs=w_tile[:, j, :].bitcast(FP8X4),
+                        rhs_scale=w_planes[4 * j : P, gate, load, :],
+                        start=False,
+                        stop=(first + j == X_PASSES - 1),
+                    )
+            return acc
+
+        acc_i = products(0)
+        sum_i = keep.tile([BATCH, D_H], F32)
+        gate_i = keep.tile([BATCH, D_H], F32)
+        nc.vector.tensor_tensor(out=sum_i[:], in0=acc_i[:], in1=bias[:, 0, :], op=ADD)
+        nc.scalar.activation(out=gate_i[:], in_=sum_i[:], func=EXP)
+
+        acc_f = products(1)
+        sum_f = keep.tile([BATCH, D_H], F32)
+        gate_f = keep.tile([BATCH, D_H], F32)
+        n_new = keep.tile([BATCH, D_H], F32)
+        kept_c = keep.tile([BATCH, D_H], F32)
+        nc.vector.tensor_tensor(out=sum_f[:], in0=acc_f[:], in1=bias[:, 1, :], op=ADD)
+        nc.scalar.activation(out=gate_f[:], in_=sum_f[:], func=EXP)
+        nc.vector.tensor_tensor(out=n_new[:], in0=gate_f[:], in1=n_old[:], op=MULT)
+        nc.vector.tensor_tensor(out=n_new[:], in0=n_new[:], in1=gate_i[:], op=ADD)
+        nc.scalar.dma_start(out=out_1[:, :], in_=n_new[:])
+        nc.vector.tensor_tensor(out=kept_c[:], in0=gate_f[:], in1=c_old[:], op=MULT)
+
+        acc_z = products(2)
+        sum_z = keep.tile([BATCH, D_H], F32)
+        gate_z = keep.tile([BATCH, D_H], F32)
+        c_new = keep.tile([BATCH, D_H], F32)
+        halves = (slice(0, HALF), slice(HALF, D_H))
+        for cols in halves:
+            nc.vector.tensor_tensor(out=sum_z[:, cols], in0=acc_z[:, cols], in1=bias[:, 2, cols], op=ADD)
+            nc.scalar.activation(out=gate_z[:, cols], in_=sum_z[:, cols], func=TANH)
+        for cols in halves:
+            nc.vector.tensor_tensor(out=c_new[:, cols], in0=gate_z[:, cols], in1=gate_i[:, cols], op=MULT)
+            nc.vector.tensor_tensor(out=c_new[:, cols], in0=c_new[:, cols], in1=kept_c[:, cols], op=ADD)
+            nc.sync.dma_start(out=out_0[:, cols], in_=c_new[:, cols])

@@ -26,6 +26,8 @@ LOADS = X_PASSES // PASSES_PER_LOAD
 WORDS_PER_PASS = K_PASS // 2
 W_BUFFERS = 12
 HALF = D_H // 2
+SCALE_ROWS = K_PASS // 32
+SMALL_PER_BIG = 2
 
 FLOPS = 2 * BATCH * (D_IN + D_H) * D_H * GATES
 
@@ -72,34 +74,57 @@ def tile_slstmcell_pa_k_kernel(
 
         w_planes = keep.tile([P, GATES, LOADS, D_H], U8, align_bytes=64)
         u_planes = keep.tile([P, D_H], U8, align_bytes=64)
-        nc.vector.memset(u_planes[:].bitcast(I32), 0)
-        for gate in range(GATES):
-            nc.vector.memset(w_planes[:, gate, :, :].bitcast(I32), 0)
-
         bias_rows = keep.tile([P, GATES, D_H], BF16)
         ones = keep.tile([P, P], BF16)
+        for gate in range(GATES):
+            nc.vector.memset(w_planes[:, gate, :, :].bitcast(I32), 0)
+        nc.vector.memset(u_planes[:].bitcast(I32), 0)
         nc.vector.memset(bias_rows[:], 0.0)
         nc.vector.memset(ones[:], 1.0)
 
         identity = keep.tile([P, P], F32)
         make_identity(nc, identity[:])
 
+        def w_scale_row(gate, q, view):
+            first = 32 * (q // 4) + q % 4
+            return (
+                w_planes[first : first + 16 : 4, gate, :, :].bitcast(view),
+                w_scales[gate][:, q, :].rearrange("(s j) n -> j s n", j=PASSES_PER_LOAD).bitcast(view),
+            )
+
+        for gate in (1, 2):
+            for q in range(SCALE_ROWS):
+                plane_rows, scale_row = w_scale_row(gate, q, F32)
+                nc.gpsimd.dma_start(out=plane_rows, in_=scale_row)
+
+        c_old = keep.tile([BATCH, D_H], BF16)
+        n_old = keep.tile([BATCH, D_H], BF16)
+        u_tile = keep.tile([P, GATES, 4 * D_H], U8, align_bytes=64)
+
+        small_loads = [w_scale_row(0, q, I32) for q in range(SCALE_ROWS)]
         for gate in range(GATES):
+            small_loads.append((bias_rows[0:1, gate, :], biases[gate].rearrange("(o n) -> o n", o=1)))
             for quad in range(4):
                 first = 32 * quad + 4 * gate
-                nc.gpsimd.dma_start(
-                    out=u_planes[first : first + 4, :].bitcast(F32),
-                    in_=u_scales[gate][0, 4 * quad : 4 * quad + 4, :].bitcast(F32),
-                )
-            for quad in range(4):
-                for row in range(4):
-                    first = 32 * quad + row
-                    nc.gpsimd.dma_start(
-                        out=w_planes[first : first + 16 : 4, gate, :, :].bitcast(F32),
-                        in_=w_scales[gate][:, 4 * quad + row, :]
-                        .rearrange("(s j) n -> j s n", j=PASSES_PER_LOAD)
-                        .bitcast(F32),
+                small_loads.append(
+                    (
+                        u_planes[first : first + 4, :].bitcast(I32),
+                        u_scales[gate][0, 4 * quad : 4 * quad + 4, :].bitcast(I32),
                     )
+                )
+            small_loads.append(
+                (
+                    u_tile[:, gate, :].bitcast(I32),
+                    u_words[gate][0].rearrange("p n t -> p (n t)").bitcast(I32),
+                )
+            )
+        small_loads.append((n_old[:], n_prev[:, :]))
+        small_loads.append((c_old[:], c_prev[:, :]))
+
+        def big_load(number, out, in_):
+            nc.sync.dma_start(out=out, in_=in_)
+            for small_out, small_in in small_loads[SMALL_PER_BIG * number : SMALL_PER_BIG * (number + 1)]:
+                nc.sync.dma_start(out=small_out, in_=small_in)
 
         h_rows = keep.tile([BATCH, D_H], BF16)
         nc.sync.dma_start(out=h_rows[:], in_=h_prev[:, :])
@@ -107,22 +132,8 @@ def tile_slstmcell_pa_k_kernel(
         for load in range(LOADS):
             rows = x_pool.tile([BATCH, PASSES_PER_LOAD * K_PASS], BF16, name="rows")
             first = load * PASSES_PER_LOAD * K_PASS
-            nc.sync.dma_start(out=rows[:], in_=x[:, first : first + PASSES_PER_LOAD * K_PASS])
+            big_load(load, rows[:], x[:, first : first + PASSES_PER_LOAD * K_PASS])
             x_rows.append(rows)
-        for gate in range(GATES):
-            nc.sync.dma_start(
-                out=bias_rows[0:1, gate, :], in_=biases[gate].rearrange("(o n) -> o n", o=1)
-            )
-        c_old = keep.tile([BATCH, D_H], BF16)
-        n_old = keep.tile([BATCH, D_H], BF16)
-        nc.sync.dma_start(out=c_old[:], in_=c_prev[:, :])
-        nc.sync.dma_start(out=n_old[:], in_=n_prev[:, :])
-        u_tile = keep.tile([P, GATES, 4 * D_H], U8, align_bytes=64)
-        for gate in range(GATES):
-            nc.sync.dma_start(
-                out=u_tile[:, gate, :].bitcast(I32),
-                in_=u_words[gate][0].rearrange("p n t -> p (n t)").bitcast(I32),
-            )
 
         h_codes = keep.tile([P, BATCH], U32, align_bytes=64)
         h_plane = keep.tile([P, BATCH], U8, align_bytes=64)
@@ -164,31 +175,34 @@ def tile_slstmcell_pa_k_kernel(
         quantise(*waiting)
 
         bias = keep.tile([BATCH, GATES, D_H], F32)
-        for gate in range(GATES):
-            spread = bank_pool.tile([BATCH, D_H], F32, tag="bank")
-            nc.tensor.matmul(spread[:], lhsT=ones[:], rhs=bias_rows[:, gate, :], start=True, stop=True)
-            nc.scalar.copy(out=bias[:, gate, :], in_=spread[:])
 
         def products(gate):
             acc = acc_pool.tile([BATCH, D_H], F32, tag="acc")
-            nc.tensor.matmul_mx(
-                out=acc[:],
-                lhsT=h_codes[:].bitcast(FP8X4),
-                lhsT_scale=h_plane[:],
-                rhs=u_tile[:, gate, :].bitcast(FP8X4),
-                rhs_scale=u_planes[4 * gate : P, :],
-                start=True,
-                stop=False,
-            )
             for load in range(LOADS):
                 w_tile = w_pool.tile([P, PASSES_PER_LOAD, 4 * D_H], U8, align_bytes=64)
                 first = load * PASSES_PER_LOAD
-                nc.sync.dma_start(
-                    out=w_tile[:].bitcast(I32),
-                    in_=w_words[gate][first : first + PASSES_PER_LOAD]
+                big_load(
+                    LOADS * (1 + gate) + load,
+                    w_tile[:].bitcast(I32),
+                    w_words[gate][first : first + PASSES_PER_LOAD]
                     .rearrange("g p n t -> p g (n t)")
                     .bitcast(I32),
                 )
+                if load == LOADS - 1:
+                    nc.tensor.matmul_mx(
+                        out=acc[:],
+                        lhsT=h_codes[:].bitcast(FP8X4),
+                        lhsT_scale=h_plane[:],
+                        rhs=u_tile[:, gate, :].bitcast(FP8X4),
+                        rhs_scale=u_planes[4 * gate : P, :],
+                        start=False,
+                        stop=False,
+                    )
+                    spread = bank_pool.tile([BATCH, D_H], F32, tag="bank")
+                    nc.tensor.matmul(
+                        spread[:], lhsT=ones[:], rhs=bias_rows[:, gate, :], start=True, stop=True
+                    )
+                    nc.scalar.copy(out=bias[:, gate, :], in_=spread[:])
                 for j in range(PASSES_PER_LOAD):
                     nc.tensor.matmul_mx(
                         out=acc[:],
@@ -196,7 +210,7 @@ def tile_slstmcell_pa_k_kernel(
                         lhsT_scale=x_planes[:, first + j, :],
                         rhs=w_tile[:, j, :].bitcast(FP8X4),
                         rhs_scale=w_planes[4 * j : P, gate, load, :],
-                        start=False,
+                        start=(first + j == 0),
                         stop=(first + j == X_PASSES - 1),
                     )
             return acc

@@ -72,13 +72,19 @@ def tile_slstmcell_pa_k_kernel(
         bank_pool = ctx.enter_context(tc.psum_pool(name="bank_pool", bufs=4))
         acc_pool = ctx.enter_context(tc.psum_pool(name="acc_pool", bufs=GATES))
 
-        w_planes = keep.tile([P, GATES, LOADS, D_H], U8, align_bytes=64)
-        u_planes = keep.tile([P, D_H], U8, align_bytes=64)
+        w_planes = []
+        u_planes = []
+        u_tiles = []
+        for gate in range(GATES):
+            w_planes.append(keep.tile([P, LOADS, D_H], U8, align_bytes=64, name="w_planes_%d" % gate))
+            u_planes.append(keep.tile([P, D_H], U8, align_bytes=64, name="u_plane_%d" % gate))
+            u_tiles.append(keep.tile([P, 4 * D_H], U8, align_bytes=64, name="u_tile_%d" % gate))
         bias_rows = keep.tile([P, GATES, D_H], BF16)
         ones = keep.tile([P, P], BF16)
         for gate in range(GATES):
-            nc.vector.memset(w_planes[:, gate, :, :].bitcast(I32), 0)
-        nc.vector.memset(u_planes[:].bitcast(I32), 0)
+            nc.vector.memset(w_planes[gate][:].bitcast(I32), 0)
+        for gate in range(GATES):
+            nc.vector.memset(u_planes[gate][:].bitcast(I32), 0)
         nc.vector.memset(bias_rows[:], 0.0)
         nc.vector.memset(ones[:], 1.0)
 
@@ -88,7 +94,7 @@ def tile_slstmcell_pa_k_kernel(
         def w_scale_row(gate, q, view):
             first = 32 * (q // 4) + q % 4
             return (
-                w_planes[first : first + 16 : 4, gate, :, :].bitcast(view),
+                w_planes[gate][first : first + 16 : 4, :, :].bitcast(view),
                 w_scales[gate][:, q, :].rearrange("(s j) n -> j s n", j=PASSES_PER_LOAD).bitcast(view),
             )
 
@@ -99,22 +105,20 @@ def tile_slstmcell_pa_k_kernel(
 
         c_old = keep.tile([BATCH, D_H], BF16)
         n_old = keep.tile([BATCH, D_H], BF16)
-        u_tile = keep.tile([P, GATES, 4 * D_H], U8, align_bytes=64)
 
         small_loads = [w_scale_row(0, q, I32) for q in range(SCALE_ROWS)]
         for gate in range(GATES):
             small_loads.append((bias_rows[0:1, gate, :], biases[gate].rearrange("(o n) -> o n", o=1)))
             for quad in range(4):
-                first = 32 * quad + 4 * gate
                 small_loads.append(
                     (
-                        u_planes[first : first + 4, :].bitcast(I32),
+                        u_planes[gate][32 * quad : 32 * quad + 4, :].bitcast(I32),
                         u_scales[gate][0, 4 * quad : 4 * quad + 4, :].bitcast(I32),
                     )
                 )
             small_loads.append(
                 (
-                    u_tile[:, gate, :].bitcast(I32),
+                    u_tiles[gate][:].bitcast(I32),
                     u_words[gate][0].rearrange("p n t -> p (n t)").bitcast(I32),
                 )
             )
@@ -193,8 +197,8 @@ def tile_slstmcell_pa_k_kernel(
                         out=acc[:],
                         lhsT=h_codes[:].bitcast(FP8X4),
                         lhsT_scale=h_plane[:],
-                        rhs=u_tile[:, gate, :].bitcast(FP8X4),
-                        rhs_scale=u_planes[4 * gate : P, :],
+                        rhs=u_tiles[gate][:].bitcast(FP8X4),
+                        rhs_scale=u_planes[gate][:],
                         start=False,
                         stop=False,
                     )
@@ -209,7 +213,7 @@ def tile_slstmcell_pa_k_kernel(
                         lhsT=x_codes[:, first + j, :].bitcast(FP8X4),
                         lhsT_scale=x_planes[:, first + j, :],
                         rhs=w_tile[:, j, :].bitcast(FP8X4),
-                        rhs_scale=w_planes[4 * j : P, gate, load, :],
+                        rhs_scale=w_planes[gate][4 * j : P, load, :],
                         start=(first + j == 0),
                         stop=(first + j == X_PASSES - 1),
                     )

@@ -183,15 +183,21 @@ def tile_slstmcell_pa_k_kernel(
         def products(gate):
             acc = acc_pool.tile([BATCH, D_H], F32, tag="acc")
             for load in range(LOADS):
-                w_tile = w_pool.tile([P, PASSES_PER_LOAD, 4 * D_H], U8, align_bytes=64)
                 first = load * PASSES_PER_LOAD
-                big_load(
-                    LOADS * (1 + gate) + load,
-                    w_tile[:].bitcast(I32),
-                    w_words[gate][first : first + PASSES_PER_LOAD]
-                    .rearrange("g p n t -> p g (n t)")
-                    .bitcast(I32),
-                )
+                pieces = PASSES_PER_LOAD if (gate == GATES - 1 and load == LOADS - 1) else 1
+                per_piece = PASSES_PER_LOAD // pieces
+                w_parts = []
+                for piece in range(pieces):
+                    w_tile = w_pool.tile([P, per_piece, 4 * D_H], U8, align_bytes=64)
+                    start = first + piece * per_piece
+                    big_load(
+                        LOADS * (1 + gate) + load + piece,
+                        w_tile[:].bitcast(I32),
+                        w_words[gate][start : start + per_piece]
+                        .rearrange("g p n t -> p g (n t)")
+                        .bitcast(I32),
+                    )
+                    w_parts.extend([(w_tile, j) for j in range(per_piece)])
                 if load == LOADS - 1:
                     nc.tensor.matmul_mx(
                         out=acc[:],
@@ -212,7 +218,7 @@ def tile_slstmcell_pa_k_kernel(
                         out=acc[:],
                         lhsT=x_codes[:, first + j, :].bitcast(FP8X4),
                         lhsT_scale=x_planes[:, first + j, :],
-                        rhs=w_tile[:, j, :].bitcast(FP8X4),
+                        rhs=w_parts[j][0][:, w_parts[j][1], :].bitcast(FP8X4),
                         rhs_scale=w_planes[gate][4 * j : P, load, :],
                         start=(first + j == 0),
                         stop=(first + j == X_PASSES - 1),
@@ -247,5 +253,6 @@ def tile_slstmcell_pa_k_kernel(
             nc.scalar.activation(out=gate_z[:, cols], in_=sum_z[:, cols], func=TANH)
         for cols in halves:
             nc.vector.tensor_tensor(out=c_new[:, cols], in0=gate_z[:, cols], in1=gate_i[:, cols], op=MULT)
+        for cols in halves:
             nc.vector.tensor_tensor(out=c_new[:, cols], in0=c_new[:, cols], in1=kept_c[:, cols], op=ADD)
             nc.sync.dma_start(out=out_0[:, cols], in_=c_new[:, cols])

@@ -24,10 +24,15 @@ X_PASSES = D_IN // K_PASS
 PASSES_PER_LOAD = 4
 LOADS = X_PASSES // PASSES_PER_LOAD
 WORDS_PER_PASS = K_PASS // 2
-W_BUFFERS = 12
+W_BUFFERS = 24
+TILE_PASSES = 2
+PLAN = ((TILE_PASSES,),) * 16
+LAST_PLAN = ((TILE_PASSES,),) * 14 + ((1,),) * 4
+H_BEFORE = 28
 HALF = D_H // 2
 SCALE_ROWS = K_PASS // 32
-SMALL_PER_BIG = 2
+SMALL_PER_X = 2
+SMALL_PER_W = 1
 
 FLOPS = 2 * BATCH * (D_IN + D_H) * D_H * GATES
 
@@ -125,9 +130,9 @@ def tile_slstmcell_pa_k_kernel(
         small_loads.append((n_old[:], n_prev[:, :]))
         small_loads.append((c_old[:], c_prev[:, :]))
 
-        def big_load(number, out, in_):
+        def big_load(out, in_, first_small, smalls):
             nc.sync.dma_start(out=out, in_=in_)
-            for small_out, small_in in small_loads[SMALL_PER_BIG * number : SMALL_PER_BIG * (number + 1)]:
+            for small_out, small_in in small_loads[first_small : first_small + smalls]:
                 nc.sync.dma_start(out=small_out, in_=small_in)
 
         h_rows = keep.tile([BATCH, D_H], BF16)
@@ -136,7 +141,7 @@ def tile_slstmcell_pa_k_kernel(
         for load in range(LOADS):
             rows = x_pool.tile([BATCH, PASSES_PER_LOAD * K_PASS], BF16, name="rows")
             first = load * PASSES_PER_LOAD * K_PASS
-            big_load(load, rows[:], x[:, first : first + PASSES_PER_LOAD * K_PASS])
+            big_load(rows[:], x[:, first : first + PASSES_PER_LOAD * K_PASS], SMALL_PER_X * load, SMALL_PER_X)
             x_rows.append(rows)
 
         h_codes = keep.tile([P, BATCH], U32, align_bytes=64)
@@ -180,25 +185,24 @@ def tile_slstmcell_pa_k_kernel(
 
         bias = keep.tile([BATCH, GATES, D_H], F32)
 
-        def products(gate):
+        def products(gate, number, plan):
             acc = acc_pool.tile([BATCH, D_H], F32, tag="acc")
-            for load in range(LOADS):
-                first = load * PASSES_PER_LOAD
-                pieces = PASSES_PER_LOAD if (gate == GATES - 1 and load == LOADS - 1) else 1
-                per_piece = PASSES_PER_LOAD // pieces
-                w_parts = []
-                for piece in range(pieces):
-                    w_tile = w_pool.tile([P, per_piece, 4 * D_H], U8, align_bytes=64)
-                    start = first + piece * per_piece
+            first = 0
+            for loads in plan:
+                w_tile = w_pool.tile([P, sum(loads), 4 * D_H], U8, align_bytes=64)
+                at = 0
+                for passes in loads:
                     big_load(
-                        LOADS * (1 + gate) + load + piece,
-                        w_tile[:].bitcast(I32),
-                        w_words[gate][start : start + per_piece]
+                        w_tile[:, at : at + passes, :].bitcast(I32),
+                        w_words[gate][first + at : first + at + passes]
                         .rearrange("g p n t -> p g (n t)")
                         .bitcast(I32),
+                        SMALL_PER_X * LOADS + SMALL_PER_W * number,
+                        SMALL_PER_W,
                     )
-                    w_parts.extend([(w_tile, j) for j in range(per_piece)])
-                if load == LOADS - 1:
+                    number += 1
+                    at += passes
+                if first == H_BEFORE:
                     nc.tensor.matmul_mx(
                         out=acc[:],
                         lhsT=h_codes[:].bitcast(FP8X4),
@@ -213,25 +217,27 @@ def tile_slstmcell_pa_k_kernel(
                         spread[:], lhsT=ones[:], rhs=bias_rows[:, gate, :], start=True, stop=True
                     )
                     nc.scalar.copy(out=bias[:, gate, :], in_=spread[:])
-                for j in range(PASSES_PER_LOAD):
+                for j in range(sum(loads)):
+                    g = first + j
                     nc.tensor.matmul_mx(
                         out=acc[:],
-                        lhsT=x_codes[:, first + j, :].bitcast(FP8X4),
-                        lhsT_scale=x_planes[:, first + j, :],
-                        rhs=w_parts[j][0][:, w_parts[j][1], :].bitcast(FP8X4),
-                        rhs_scale=w_planes[gate][4 * j : P, load, :],
-                        start=(first + j == 0),
-                        stop=(first + j == X_PASSES - 1),
+                        lhsT=x_codes[:, g, :].bitcast(FP8X4),
+                        lhsT_scale=x_planes[:, g, :],
+                        rhs=w_tile[:, j, :].bitcast(FP8X4),
+                        rhs_scale=w_planes[gate][4 * (g % PASSES_PER_LOAD) : P, g // PASSES_PER_LOAD, :],
+                        start=(g == 0),
+                        stop=(g == X_PASSES - 1),
                     )
-            return acc
+                first += sum(loads)
+            return acc, number
 
-        acc_i = products(0)
+        acc_i, number = products(0, 0, PLAN)
         sum_i = keep.tile([BATCH, D_H], F32)
         gate_i = keep.tile([BATCH, D_H], F32)
         nc.vector.tensor_tensor(out=sum_i[:], in0=acc_i[:], in1=bias[:, 0, :], op=ADD)
         nc.scalar.activation(out=gate_i[:], in_=sum_i[:], func=EXP)
 
-        acc_f = products(1)
+        acc_f, number = products(1, number, PLAN)
         sum_f = keep.tile([BATCH, D_H], F32)
         gate_f = keep.tile([BATCH, D_H], F32)
         n_new = keep.tile([BATCH, D_H], F32)
@@ -243,7 +249,7 @@ def tile_slstmcell_pa_k_kernel(
         nc.scalar.dma_start(out=out_1[:, :], in_=n_new[:])
         nc.vector.tensor_tensor(out=kept_c[:], in0=gate_f[:], in1=c_old[:], op=MULT)
 
-        acc_z = products(2)
+        acc_z, number = products(2, number, LAST_PLAN)
         sum_z = keep.tile([BATCH, D_H], F32)
         gate_z = keep.tile([BATCH, D_H], F32)
         c_new = keep.tile([BATCH, D_H], F32)

@@ -27,8 +27,9 @@ WORDS_PER_PASS = K_PASS // 2
 W_BUFFERS = 24
 TILE_PASSES = 2
 PLAN = ((TILE_PASSES,),) * 16
-LAST_PLAN = ((TILE_PASSES,),) * 14 + ((1,),) * 4
-H_BEFORE = 28
+END_PASSES = 4
+LAST_PLAN = ((TILE_PASSES,),) * ((X_PASSES - END_PASSES) // TILE_PASSES)
+QUARTER = D_H // 4
 HALF = D_H // 2
 SCALE_ROWS = K_PASS // 32
 SMALL_PER_X = 2
@@ -185,8 +186,9 @@ def tile_slstmcell_pa_k_kernel(
 
         bias = keep.tile([BATCH, GATES, D_H], F32)
 
-        def products(gate, number, plan):
+        def products(gate, number, plan, h_before):
             acc = acc_pool.tile([BATCH, D_H], F32, tag="acc")
+            covered = sum([sum(loads) for loads in plan])
             first = 0
             for loads in plan:
                 w_tile = w_pool.tile([P, sum(loads), 4 * D_H], U8, align_bytes=64)
@@ -202,7 +204,7 @@ def tile_slstmcell_pa_k_kernel(
                     )
                     number += 1
                     at += passes
-                if first == H_BEFORE:
+                if first == h_before:
                     nc.tensor.matmul_mx(
                         out=acc[:],
                         lhsT=h_codes[:].bitcast(FP8X4),
@@ -226,18 +228,18 @@ def tile_slstmcell_pa_k_kernel(
                         rhs=w_tile[:, j, :].bitcast(FP8X4),
                         rhs_scale=w_planes[gate][4 * (g % PASSES_PER_LOAD) : P, g // PASSES_PER_LOAD, :],
                         start=(g == 0),
-                        stop=(g == X_PASSES - 1),
+                        stop=(g == covered - 1),
                     )
                 first += sum(loads)
             return acc, number
 
-        acc_i, number = products(0, 0, PLAN)
+        acc_i, number = products(0, 0, PLAN, X_PASSES - 4)
         sum_i = keep.tile([BATCH, D_H], F32)
         gate_i = keep.tile([BATCH, D_H], F32)
         nc.vector.tensor_tensor(out=sum_i[:], in0=acc_i[:], in1=bias[:, 0, :], op=ADD)
         nc.scalar.activation(out=gate_i[:], in_=sum_i[:], func=EXP)
 
-        acc_f, number = products(1, number, PLAN)
+        acc_f, number = products(1, number, PLAN, X_PASSES - 4)
         sum_f = keep.tile([BATCH, D_H], F32)
         gate_f = keep.tile([BATCH, D_H], F32)
         n_new = keep.tile([BATCH, D_H], F32)
@@ -249,16 +251,64 @@ def tile_slstmcell_pa_k_kernel(
         nc.scalar.dma_start(out=out_1[:, :], in_=n_new[:])
         nc.vector.tensor_tensor(out=kept_c[:], in0=gate_f[:], in1=c_old[:], op=MULT)
 
-        acc_z, number = products(2, number, LAST_PLAN)
+        acc_z, number = products(2, number, LAST_PLAN, TILE_PASSES)
+        end_first = X_PASSES - END_PASSES
+        w_end = keep.tile([P, END_PASSES, 4 * D_H], U8, align_bytes=64)
+        end_source = w_words[2][end_first:X_PASSES].rearrange("g p n t -> p g (n t)")
+        for q in range(4):
+            word_cols = slice(4 * q * QUARTER, 4 * (q + 1) * QUARTER)
+            nc.sync.dma_start(
+                out=w_end[:, :, word_cols].bitcast(I32), in_=end_source[:, :, word_cols].bitcast(I32)
+            )
+        before_z = keep.tile([BATCH, D_H], F32)
+        nc.vector.tensor_tensor(out=before_z[:], in0=acc_z[:], in1=bias[:, 2, :], op=ADD)
+        end_banks = []
+        for q in range(4):
+            end_bank = bank_pool.tile([BATCH, QUARTER], F32, tag="bank")
+            for j in range(END_PASSES):
+                g = end_first + j
+                nc.tensor.matmul_mx(
+                    out=end_bank[:],
+                    lhsT=x_codes[:, g, :].bitcast(FP8X4),
+                    lhsT_scale=x_planes[:, g, :],
+                    rhs=w_end[:, j, 4 * q * QUARTER : 4 * (q + 1) * QUARTER].bitcast(FP8X4),
+                    rhs_scale=w_planes[2][
+                        4 * (g % PASSES_PER_LOAD) : P, g // PASSES_PER_LOAD, q * QUARTER : (q + 1) * QUARTER
+                    ],
+                    start=(j == 0),
+                    stop=(j == END_PASSES - 1),
+                )
+            end_banks.append(end_bank)
         sum_z = keep.tile([BATCH, D_H], F32)
         gate_z = keep.tile([BATCH, D_H], F32)
         c_new = keep.tile([BATCH, D_H], F32)
-        halves = (slice(0, HALF), slice(HALF, D_H))
-        for cols in halves:
-            nc.vector.tensor_tensor(out=sum_z[:, cols], in0=acc_z[:, cols], in1=bias[:, 2, cols], op=ADD)
+
+        def cols_of(q):
+            return slice(q * QUARTER, (q + 1) * QUARTER)
+
+        def squash(q):
+            cols = cols_of(q)
+            nc.vector.tensor_tensor(out=sum_z[:, cols], in0=end_banks[q][:], in1=before_z[:, cols], op=ADD)
             nc.scalar.activation(out=gate_z[:, cols], in_=sum_z[:, cols], func=TANH)
-        for cols in halves:
+
+        def product(q):
+            cols = cols_of(q)
             nc.vector.tensor_tensor(out=c_new[:, cols], in0=gate_z[:, cols], in1=gate_i[:, cols], op=MULT)
-        for cols in halves:
+
+        def finish(q):
+            cols = cols_of(q)
             nc.vector.tensor_tensor(out=c_new[:, cols], in0=c_new[:, cols], in1=kept_c[:, cols], op=ADD)
             nc.sync.dma_start(out=out_0[:, cols], in_=c_new[:, cols])
+
+        squash(0)
+        squash(1)
+        product(0)
+        squash(2)
+        finish(0)
+        product(1)
+        squash(3)
+        finish(1)
+        product(2)
+        product(3)
+        finish(2)
+        finish(3)

from contextlib import ExitStack

import concourse.mybir as mybir
from concourse.masks import make_identity

F32 = mybir.dt.float32
BF16 = mybir.dt.bfloat16
I32 = mybir.dt.int32
U32 = mybir.dt.uint32
U8 = mybir.dt.uint8
FP8X4 = mybir.dt.float8_e4m3fn_x4
ADD = mybir.AluOpType.add
MULT = mybir.AluOpType.mult
EXP = mybir.ActivationFunctionType.Exp
TANH = mybir.ActivationFunctionType.Tanh

P = 128
BATCH = 128
D_IN = 16384
D_H = 512
GATES = 3
K_PASS = 4 * P
X_PASSES = D_IN // K_PASS
PASSES_PER_LOAD = 4
LOADS = X_PASSES // PASSES_PER_LOAD
WORDS_PER_PASS = K_PASS // 2
W_BUFFERS = 24
TILE_PASSES = 2
PLAN = ((TILE_PASSES,),) * 16
END_PASSES = 4
LAST_PLAN = ((TILE_PASSES,),) * ((X_PASSES - END_PASSES) // TILE_PASSES)
QUARTER = D_H // 4
HALF = D_H // 2
SCALE_ROWS = K_PASS // 32
SMALL_PER_X = 2
SMALL_PER_W = 1

FLOPS = 2 * BATCH * (D_IN + D_H) * D_H * GATES


def tile_slstmcell_pa_k_kernel(
    tc,
    x,
    h_prev,
    c_prev,
    n_prev,
    W_i_words,
    W_i_scales,
    b_i,
    U_i_words,
    U_i_scales,
    W_f_words,
    W_f_scales,
    b_f,
    U_f_words,
    U_f_scales,
    W_z_words,
    W_z_scales,
    b_z,
    U_z_words,
    U_z_scales,
    out_0,
    out_1,
):
    nc = tc.nc
    w_words = (W_i_words, W_f_words, W_z_words)
    w_scales = (W_i_scales, W_f_scales, W_z_scales)
    u_words = (U_i_words, U_f_words, U_z_words)
    u_scales = (U_i_scales, U_f_scales, U_z_scales)
    biases = (b_i, b_f, b_z)

    with ExitStack() as ctx:
        ctx.enter_context(tc.manual_schedule())
        keep = ctx.enter_context(tc.tile_pool(name="keep", bufs=1))
        x_pool = ctx.enter_context(tc.tile_pool(name="x_pool", bufs=LOADS))
        grouped_pool = ctx.enter_context(tc.tile_pool(name="grouped_pool", bufs=3))
        w_pool = ctx.enter_context(tc.tile_pool(name="w_pool", bufs=W_BUFFERS))
        bank_pool = ctx.enter_context(tc.psum_pool(name="bank_pool", bufs=4))
        acc_pool = ctx.enter_context(tc.psum_pool(name="acc_pool", bufs=GATES))

        w_planes = []
        u_planes = []
        u_tiles = []
        for gate in range(GATES):
            w_planes.append(keep.tile([P, LOADS, D_H], U8, align_bytes=64, name="w_planes_%d" % gate))
            u_planes.append(keep.tile([P, D_H], U8, align_bytes=64, name="u_plane_%d" % gate))
            u_tiles.append(keep.tile([P, 4 * D_H], U8, align_bytes=64, name="u_tile_%d" % gate))
        bias_rows = keep.tile([P, GATES, D_H], BF16)
        ones = keep.tile([P, P], BF16)
        for gate in range(GATES):
            nc.vector.memset(w_planes[gate][:].bitcast(I32), 0)
        for gate in range(GATES):
            nc.vector.memset(u_planes[gate][:].bitcast(I32), 0)
        nc.vector.memset(bias_rows[:], 0.0)
        nc.vector.memset(ones[:], 1.0)

        identity = keep.tile([P, P], F32)
        make_identity(nc, identity[:])

        def w_scale_row(gate, q, view):
            first = 32 * (q // 4) + q % 4
            return (
                w_planes[gate][first : first + 16 : 4, :, :].bitcast(view),
                w_scales[gate][:, q, :].rearrange("(s j) n -> j s n", j=PASSES_PER_LOAD).bitcast(view),
            )

        for gate in (1, 2):
            for q in range(SCALE_ROWS):
                plane_rows, scale_row = w_scale_row(gate, q, F32)
                nc.gpsimd.dma_start(out=plane_rows, in_=scale_row)

        c_old = keep.tile([BATCH, D_H], BF16)
        n_old = keep.tile([BATCH, D_H], BF16)

        small_loads = [w_scale_row(0, q, I32) for q in range(SCALE_ROWS)]
        for gate in range(GATES):
            small_loads.append((bias_rows[0:1, gate, :], biases[gate].rearrange("(o n) -> o n", o=1)))
            for quad in range(4):
                small_loads.append(
                    (
                        u_planes[gate][32 * quad : 32 * quad + 4, :].bitcast(I32),
                        u_scales[gate][0, 4 * quad : 4 * quad + 4, :].bitcast(I32),
                    )
                )
            small_loads.append(
                (
                    u_tiles[gate][:].bitcast(I32),
                    u_words[gate][0].rearrange("p n t -> p (n t)").bitcast(I32),
                )
            )
        small_loads.append((n_old[:], n_prev[:, :]))
        small_loads.append((c_old[:], c_prev[:, :]))

        def big_load(out, in_, first_small, smalls):
            nc.sync.dma_start(out=out, in_=in_)
            for small_out, small_in in small_loads[first_small : first_small + smalls]:
                nc.sync.dma_start(out=small_out, in_=small_in)

        h_rows = keep.tile([BATCH, D_H], BF16)
        nc.sync.dma_start(out=h_rows[:], in_=h_prev[:, :])
        x_rows = []
        for load in range(LOADS):
            rows = x_pool.tile([BATCH, PASSES_PER_LOAD * K_PASS], BF16, name="rows")
            first = load * PASSES_PER_LOAD * K_PASS
            big_load(rows[:], x[:, first : first + PASSES_PER_LOAD * K_PASS], SMALL_PER_X * load, SMALL_PER_X)
            x_rows.append(rows)

        h_codes = keep.tile([P, BATCH], U32, align_bytes=64)
        h_plane = keep.tile([P, BATCH], U8, align_bytes=64)
        x_codes = keep.tile([P, X_PASSES, BATCH], U32, align_bytes=64)
        x_planes = keep.tile([P, X_PASSES, BATCH], U8, align_bytes=64)

        def regroup(rows, first_pass, passes, copy, grouped_words):
            words = rows.bitcast(F32)
            bank = bank_pool.tile([P, passes, 2, BATCH], F32, tag="bank")
            for g in range(passes):
                start = (first_pass + g) * WORDS_PER_PASS
                for u in range(2):
                    nc.tensor.transpose(
                        bank[:, g, u, :], words[:, start + u : start + WORDS_PER_PASS : 2], identity[:]
                    )
            copy(
                out=grouped_words.rearrange("p (g b u) -> p g b u", g=passes, u=2),
                in_=bank[:].rearrange("p g u b -> p g b u"),
            )

        def quantise(grouped, codes, plane):
            nc.vector.quantize_mx(out=codes.bitcast(FP8X4), scales=plane, in_=grouped)

        h_grouped = keep.tile([P, K_PASS], BF16, align_bytes=64)
        regroup(h_rows[:], 0, 1, nc.vector.tensor_copy, h_grouped[:].bitcast(F32))
        waiting = (h_grouped[:], h_codes[:], h_plane[:])
        for load in range(LOADS):
            grouped = grouped_pool.tile([P, PASSES_PER_LOAD * K_PASS], BF16, align_bytes=64)
            grouped_words = grouped[:].bitcast(F32)
            regroup(x_rows[load][:], 0, 2, nc.vector.tensor_copy, grouped_words[:, 0:K_PASS])
            regroup(x_rows[load][:], 2, 2, nc.scalar.copy, grouped_words[:, K_PASS : 2 * K_PASS])
            quantise(*waiting)
            passes = slice(load * PASSES_PER_LOAD, (load + 1) * PASSES_PER_LOAD)
            waiting = (
                grouped[:],
                x_codes[:, passes, :].rearrange("p g b -> p (g b)"),
                x_planes[:, passes, :].rearrange("p g b -> p (g b)"),
            )
        quantise(*waiting)

        bias = keep.tile([BATCH, GATES, D_H], F32)

        def products(gate, number, plan, h_before):
            acc = acc_pool.tile([BATCH, D_H], F32, tag="acc")
            covered = sum([sum(loads) for loads in plan])
            first = 0
            for loads in plan:
                w_tile = w_pool.tile([P, sum(loads), 4 * D_H], U8, align_bytes=64)
                at = 0
                for passes in loads:
                    big_load(
                        w_tile[:, at : at + passes, :].bitcast(I32),
                        w_words[gate][first + at : first + at + passes]
                        .rearrange("g p n t -> p g (n t)")
                        .bitcast(I32),
                        SMALL_PER_X * LOADS + SMALL_PER_W * number,
                        SMALL_PER_W,
                    )
                    number += 1
                    at += passes
                if first == h_before:
                    nc.tensor.matmul_mx(
                        out=acc[:],
                        lhsT=h_codes[:].bitcast(FP8X4),
                        lhsT_scale=h_plane[:],
                        rhs=u_tiles[gate][:].bitcast(FP8X4),
                        rhs_scale=u_planes[gate][:],
                        start=False,
                        stop=False,
                    )
                    spread = bank_pool.tile([BATCH, D_H], F32, tag="bank")
                    nc.tensor.matmul(
                        spread[:], lhsT=ones[:], rhs=bias_rows[:, gate, :], start=True, stop=True
                    )
                    nc.scalar.copy(out=bias[:, gate, :], in_=spread[:])
                for j in range(sum(loads)):
                    g = first + j
                    nc.tensor.matmul_mx(
                        out=acc[:],
                        lhsT=x_codes[:, g, :].bitcast(FP8X4),
                        lhsT_scale=x_planes[:, g, :],
                        rhs=w_tile[:, j, :].bitcast(FP8X4),
                        rhs_scale=w_planes[gate][4 * (g % PASSES_PER_LOAD) : P, g // PASSES_PER_LOAD, :],
                        start=(g == 0),
                        stop=(g == covered - 1),
                    )
                first += sum(loads)
            return acc, number

        acc_i, number = products(0, 0, PLAN, X_PASSES - 4)
        sum_i = keep.tile([BATCH, D_H], F32)
        gate_i = keep.tile([BATCH, D_H], F32)
        nc.vector.tensor_tensor(out=sum_i[:], in0=acc_i[:], in1=bias[:, 0, :], op=ADD)
        nc.scalar.activation(out=gate_i[:], in_=sum_i[:], func=EXP)

        acc_f, number = products(1, number, PLAN, X_PASSES - 4)
        sum_f = keep.tile([BATCH, D_H], F32)
        gate_f = keep.tile([BATCH, D_H], F32)
        n_new = keep.tile([BATCH, D_H], F32)
        kept_c = keep.tile([BATCH, D_H], F32)
        nc.vector.tensor_tensor(out=sum_f[:], in0=acc_f[:], in1=bias[:, 1, :], op=ADD)
        nc.scalar.activation(out=gate_f[:], in_=sum_f[:], func=EXP)
        nc.vector.tensor_tensor(out=n_new[:], in0=gate_f[:], in1=n_old[:], op=MULT)
        nc.vector.tensor_tensor(out=n_new[:], in0=n_new[:], in1=gate_i[:], op=ADD)
        nc.scalar.dma_start(out=out_1[:, :], in_=n_new[:])
        nc.vector.tensor_tensor(out=kept_c[:], in0=gate_f[:], in1=c_old[:], op=MULT)

        acc_z, number = products(2, number, LAST_PLAN, TILE_PASSES)
        end_first = X_PASSES - END_PASSES
        w_end = keep.tile([P, END_PASSES, 4 * D_H], U8, align_bytes=64)
        end_source = w_words[2][end_first:X_PASSES].rearrange("g p n t -> p g (n t)")
        for q in range(4):
            word_cols = slice(4 * q * QUARTER, 4 * (q + 1) * QUARTER)
            nc.sync.dma_start(
                out=w_end[:, :, word_cols].bitcast(I32), in_=end_source[:, :, word_cols].bitcast(I32)
            )
        before_z = keep.tile([BATCH, D_H], F32)
        nc.vector.tensor_tensor(out=before_z[:], in0=acc_z[:], in1=bias[:, 2, :], op=ADD)
        end_banks = []
        for q in range(4):
            end_bank = bank_pool.tile([BATCH, QUARTER], F32, tag="bank")
            for j in range(END_PASSES):
                g = end_first + j
                nc.tensor.matmul_mx(
                    out=end_bank[:],
                    lhsT=x_codes[:, g, :].bitcast(FP8X4),
                    lhsT_scale=x_planes[:, g, :],
                    rhs=w_end[:, j, 4 * q * QUARTER : 4 * (q + 1) * QUARTER].bitcast(FP8X4),
                    rhs_scale=w_planes[2][
                        4 * (g % PASSES_PER_LOAD) : P, g // PASSES_PER_LOAD, q * QUARTER : (q + 1) * QUARTER
                    ],
                    start=(j == 0),
                    stop=(j == END_PASSES - 1),
                )
            end_banks.append(end_bank)
        sum_z = keep.tile([BATCH, D_H], F32)
        gate_z = keep.tile([BATCH, D_H], F32)
        c_new = keep.tile([BATCH, D_H], F32)

        def cols_of(q):
            return slice(q * QUARTER, (q + 1) * QUARTER)

        def squash(q):
            cols = cols_of(q)
            nc.vector.tensor_tensor(out=sum_z[:, cols], in0=end_banks[q][:], in1=before_z[:, cols], op=ADD)
            nc.scalar.activation(out=gate_z[:, cols], in_=sum_z[:, cols], func=TANH)

        def product(q):
            cols = cols_of(q)
            nc.vector.tensor_tensor(out=c_new[:, cols], in0=gate_z[:, cols], in1=gate_i[:, cols], op=MULT)

        def finish(q):
            cols = cols_of(q)
            nc.vector.tensor_tensor(out=c_new[:, cols], in0=c_new[:, cols], in1=kept_c[:, cols], op=ADD)
            nc.sync.dma_start(out=out_0[:, cols], in_=c_new[:, cols])

        squash(0)
        squash(1)
        product(0)
        squash(2)
        finish(0)
        product(1)
        squash(3)
        finish(1)
        product(2)
        product(3)
        finish(2)
        finish(3)
